import numpy as np
import ml_dtypes


def mxq(x, axis, fmt="e4m3"):
    dtype, down = {"e4m3": (ml_dtypes.float8_e4m3fn, 7), "e5m2": (ml_dtypes.float8_e5m2, 14)}[fmt]
    v = np.moveaxis(np.asarray(x, np.float32).astype(ml_dtypes.bfloat16).astype(np.float64), axis, -1)
    blocks = v.reshape(v.shape[:-1] + (-1, 32))
    amax = np.abs(blocks).max(-1, keepdims=True)
    byte = np.maximum(np.where(amax > 0, np.frexp(amax)[1] - 1 + 127, 0) - down, 1)
    scale = np.exp2(byte - 127.0)
    codes = (blocks / scale).astype(np.float32).astype(dtype).astype(np.float64)
    return np.moveaxis((codes * scale).reshape(v.shape), -1, axis)


WIDE = False


def mx_kscale(k):
    if not WIDE:
        return np.ones(k)
    levels = np.array([10, -10, 5, -5, 0])
    a = np.random.permutation(np.resize(levels, k // 512 * 4)).reshape(k // 512, 4)
    idx = np.arange(k)
    return np.exp2(a[idx // 512, idx % 128 // 32])


BF16 = ml_dtypes.bfloat16


def bf(x):
    return np.asarray(x, np.float32).astype(BF16)


def f64(x):
    return np.asarray(x).astype(np.float64)


M, I, O = 8192, 1024, 256
SPARSITY = 0.98


def _build_mask():
    num_connections = int((1 - SPARSITY) * I * O)
    cpn = max(1, num_connections // O)
    rows = np.arange(O)[:, None]
    cols = (rows * cpn + np.arange(cpn)[None, :]) % I
    mask = np.zeros((O, I), dtype=np.float32)
    mask[np.repeat(np.arange(O), cpn), cols.reshape(-1)] = 1.0
    return mask, cpn


def setup_inputs():
    s = mx_kscale(I)
    mask_np, cpn = _build_mask()
    return {"x": bf(np.random.standard_normal((M, I)) * s),
            "weight": bf(np.random.standard_normal((O, I)) * np.sqrt(2.0 / cpn) / s[None, :]),
            "bias": bf(np.random.standard_normal(O) * 0.1),
            "mask": bf(mask_np)}


def reference(x, weight, bias, mask):
    masked_weight = f64(weight) * f64(mask)
    return (mxq(f64(x), 1, "e4m3") @ mxq(masked_weight, 1, "e4m3").T) + f64(bias)

@@ -1,0 +1,252 @@
+from contextlib import ExitStack
+
+import concourse.mybir as mybir
+from concourse.masks import make_identity
+
+F32 = mybir.dt.float32
+BF16 = mybir.dt.bfloat16
+U32 = mybir.dt.uint32
+U8 = mybir.dt.uint8
+FP8X4 = mybir.dt.float8_e4m3fn_x4
+
+M, K, O = 8192, 1024, 256
+P = 128
+FLOPS = 2 * M * K * O
+
+CHUNKS = [2,2,4,8,8,8,8,8,8,8]
+XBIG_BUFS = 5
+MANUAL = True
+RP = 2
+LAG = 1
+QAHEAD = 3
+NT = 5
+GB = 4
+CB = 5
+WFIRST = False
+NPAIR = M // P // 2
+
+
+def merge(queues, deps):
+    pos = [0] * len(queues)
+    done = set()
+    order = []
+    total = sum(len(q) for q in queues)
+    for sweep in range(total + 1):
+        moved = False
+        for qi, q in enumerate(queues):
+            if pos[qi] < len(q):
+                op = q[pos[qi]]
+                if all(d in done for d in deps(op)):
+                    order.append(op)
+                    done.add(op)
+                    pos[qi] += 1
+                    moved = True
+        if not moved:
+            break
+    assert len(order) == total, "the four orders contradict each other"
+    return order
+
+
+def tile_structuredconnection_t_kernel(tc, x, weight, bias, mask, out):
+    nc = tc.nc
+    mult = mybir.AluOpType.mult
+    add = mybir.AluOpType.add
+    with ExitStack() as ctx:
+        const = ctx.enter_context(tc.tile_pool(name="const", bufs=1))
+        xin = ctx.enter_context(tc.tile_pool(name="xin", bufs=1))
+        stage = ctx.enter_context(tc.tile_pool(name="stage", bufs=1))
+        work = ctx.enter_context(tc.tile_pool(name="work", bufs=1))
+        ps_t = ctx.enter_context(tc.psum_pool(name="ps_t", bufs=NT))
+        ps_o = ctx.enter_context(tc.psum_pool(name="ps_o", bufs=8 - NT))
+        if MANUAL:
+            ctx.enter_context(tc.manual_schedule())
+
+        where = []
+        row0 = []
+        r = 0
+        for c, t_cnt in enumerate(CHUNKS):
+            row0.append(r)
+            r += P * t_cnt
+            for t in range(t_cnt):
+                where.append((c, t))
+        assert r == M
+
+        x_sb = []
+        o_sb = []
+        w_sb = const.tile([P, 2, K], BF16, name="w_sb")
+        m_sb = const.tile([P, 2, K], BF16, name="m_sb")
+        brow = const.tile([P, O], BF16, name="brow")
+        ones = const.tile([P, P], BF16, name="ones")
+        ident = const.tile([P, P], F32, name="ident")
+        nc.vector.memset(brow[:], 0.0)
+        nc.vector.memset(ones[:], 1.0)
+        make_identity(nc, ident[:])
+        nc.scalar.dma_start(out=brow[0:1, :], in_=bias.unsqueeze(0))
+
+        def load_w():
+            nc.sync.dma_start(out=w_sb[:], in_=weight.rearrange("(t p) k -> p t k", p=P))
+            nc.sync.dma_start(out=m_sb[:], in_=mask.rearrange("(t p) k -> p t k", p=P))
+
+        if WFIRST:
+            load_w()
+        for c, t_cnt in enumerate(CHUNKS):
+            if t_cnt == 8:
+                xt_sb = xin.tile([P, t_cnt * K], BF16, name="xbig%d" % c, tag="xbig", bufs=XBIG_BUFS)
+            else:
+                xt_sb = xin.tile([P, t_cnt * K], BF16, name="xs%d" % c, tag="xs%d" % c)
+            rows = x[row0[c] : row0[c] + P * t_cnt, :]
+            nc.sync.dma_start(out=xt_sb[:], in_=rows.rearrange("(p t) k -> p (t k)", t=t_cnt))
+            x_sb.append(xt_sb)
+            o_sb.append(stage.tile([P, t_cnt * O], F32, name="o%d" % c, tag="o%d" % c))
+            if c == 0 and not WFIRST:
+                load_w()
+
+        wm = const.tile([P, 2 * K], BF16, name="wm")
+        wg = const.tile([P, 2 * O * 4], BF16, name="wg", align_bytes=64)
+        wcodes = const.tile([P, 2 * O], U32, name="wcodes", align_bytes=64)
+        wscales = const.tile([P, 2 * O], U8, name="wscales", align_bytes=64)
+        bias2 = const.tile([P, 2, O], F32, name="bias2")
+        wg32 = wg[:].bitcast(F32).rearrange("p (g o u) -> p g o u", g=2, u=2)
+
+        bank = {}
+        grp = {}
+        codes = {}
+        scl = {}
+        acc = {}
+
+        def transposes(key, src32, col0):
+            pt = ps_t.tile([P, 4, P], F32, name="pt", tag="pt")
+            bank[key] = pt
+            for q in range(4):
+                nc.tensor.transpose(pt[:, q, :], src32[:, col0 + q * P : col0 + (q + 1) * P], ident[:])
+
+        def op_t(n):
+            c, t = where[n]
+            transposes(("x", n), x_sb[c][:].bitcast(F32), t * (K // 2))
+
+        def op_c(n):
+            h, i = divmod(n, 2)
+            if i == 0:
+                grp[h] = work.tile([P, 2 * K], BF16, name="grp", tag="grp", bufs=GB, align_bytes=64)
+            dst = grp[h][:].bitcast(F32)[:, i * (K // 2) : (i + 1) * (K // 2)]
+            nc.scalar.copy(
+                out=dst.rearrange("p (g r u) -> p g r u", g=2, u=2),
+                in_=bank[("x", n)][:].rearrange("p (g u) r -> p g r u", u=2),
+            )
+
+        def op_q(h):
+            codes[h] = work.tile([P, K // 2], U32, name="codes", tag="codes", bufs=CB, align_bytes=64)
+            scl[h] = work.tile([P, K // 2], U8, name="scl", tag="scl", bufs=CB, align_bytes=64)
+            nc.vector.quantize_mx(out=codes[h][:].bitcast(FP8X4), scales=scl[h][:], in_=grp[h][:])
+
+        def op_x(h):
+            acc[h] = ps_o.tile([P, 2, O], F32, name="acc", tag="acc")
+            for i in range(2):
+                for g in range(2):
+                    lo = (i * 2 + g) * P
+                    nc.tensor.matmul_mx(
+                        out=acc[h][:, i, :],
+                        lhsT=codes[h][:, lo : lo + P].bitcast(FP8X4),
+                        lhsT_scale=scl[h][:, lo : lo + P],
+                        rhs=wcodes[:, g * O : (g + 1) * O].bitcast(FP8X4),
+                        rhs_scale=wscales[:, g * O : (g + 1) * O],
+                        start=(g == 0),
+                        stop=(g == 1),
+                    )
+
+        def op_a(h):
+            c, t = where[2 * h]
+            nc.vector.tensor_tensor(
+                out=o_sb[c][:, t * O : (t + 2) * O],
+                in0=acc[h][:].rearrange("p i o -> p (i o)"),
+                in1=bias2[:].rearrange("p i o -> p (i o)"),
+                op=add,
+            )
+
+        def op_s(c):
+            t_cnt = CHUNKS[c]
+            rows = out[row0[c] : row0[c] + P * t_cnt, :]
+            nc.sync.dma_start(out=rows.rearrange("(p t) o -> p (t o)", t=t_cnt), in_=o_sb[c][:])
+
+        def op_wm(t):
+            nc.vector.tensor_tensor(out=wm[:, t * K : (t + 1) * K], in0=w_sb[:, t, :], in1=m_sb[:, t, :], op=mult)
+
+        def op_tw(t):
+            transposes(("w", t), wm[:].bitcast(F32), t * (K // 2))
+
+        def op_cw(t):
+            nc.scalar.copy(
+                out=wg32[:, :, t * P : (t + 1) * P, :],
+                in_=bank[("w", t)][:].rearrange("p (g u) r -> p g r u", u=2),
+            )
+
+        def op_qw(z):
+            nc.vector.quantize_mx(out=wcodes[:].bitcast(FP8X4), scales=wscales[:], in_=wg[:])
+
+        def op_bm(z):
+            acc["b"] = ps_o.tile([P, 2, O], F32, name="acc", tag="acc")
+            nc.tensor.matmul(acc["b"][:, 0, :], lhsT=ones[:], rhs=brow[:], start=True, stop=True)
+
+        def op_bc(z):
+            for i in range(2):
+                nc.vector.tensor_copy(out=bias2[:, i, :], in_=acc["b"][:, 0, :])
+
+        emit = {"T": op_t, "C": op_c, "Q": op_q, "X": op_x, "A": op_a, "S": op_s,
+                "WM": op_wm, "TW": op_tw, "CW": op_cw, "QW": op_qw, "BM": op_bm, "BC": op_bc}
+
+        pairs_of = [[h for h in range(NPAIR) if where[2 * h][0] == c] for c in range(len(CHUNKS))]
+
+        def deps(op):
+            kind, v = op
+            if kind == "C":
+                return [("T", v)]
+            if kind == "Q":
+                return [("C", 2 * v), ("C", 2 * v + 1)]
+            if kind == "X":
+                return [("Q", v), ("QW", 0)]
+            if kind == "A":
+                return [("X", v), ("BC", 0)]
+            if kind == "S":
+                return [("A", h) for h in pairs_of[v]]
+            if kind == "TW":
+                return [("WM", v)]
+            if kind == "CW":
+                return [("TW", v)]
+            if kind == "QW":
+                return [("CW", 0), ("CW", 1)]
+            if kind == "BC":
+                return [("BM", 0)]
+            return []
+
+        w_pe = [("TW", 0), ("TW", 1), ("BM", 0)]
+        w_act = [("CW", 0), ("CW", 1)]
+        nr = NPAIR // RP
+        pe = []
+        act = []
+        for s in range(nr + LAG):
+            if s < nr:
+                for n in range(2 * RP * s, 2 * RP * (s + 1)):
+                    pe.append(("T", n))
+                    act.append(("C", n))
+                    if n == 1 and not WFIRST:
+                        pe.extend(w_pe)
+                        act.extend(w_act)
+            if s >= LAG:
+                for h in range(RP * (s - LAG), RP * (s - LAG + 1)):
+                    pe.append(("X", h))
+        if WFIRST:
+            pe = w_pe + pe
+            act = w_act + act
+        dve = [("WM", 0), ("WM", 1)]
+        if not WFIRST:
+            dve.append(("Q", 0))
+        dve.extend([("QW", 0), ("BC", 0)])
+        dve.extend([("Q", h) for h in range(0 if WFIRST else 1, QAHEAD)])
+        for h in range(NPAIR):
+            dve.append(("A", h))
+            if h + QAHEAD < NPAIR:
+                dve.append(("Q", h + QAHEAD))
+        sp = [("S", c) for c in range(len(CHUNKS))]
+
+        for kind, v in merge([pe, act, dve, sp], deps):
+            emit[kind](v)

@@ -84,8 +84,8 @@ def tile_structuredconnection_t_kernel(tc, x, weight, bias, mask, out):
         nc.scalar.dma_start(out=brow[0:1, :], in_=bias.unsqueeze(0))
 
         def load_w():
-            nc.sync.dma_start(out=w_sb[:], in_=weight.rearrange("(t p) k -> p t k", p=P))
-            nc.sync.dma_start(out=m_sb[:], in_=mask.rearrange("(t p) k -> p t k", p=P))
+            nc.sync.dma_start(out=w_sb[:], in_=weight.rearrange("(p t) k -> p t k", t=2))
+            nc.sync.dma_start(out=m_sb[:], in_=mask.rearrange("(p t) k -> p t k", t=2))
 
         if WFIRST:
             load_w()
@@ -101,7 +101,6 @@ def tile_structuredconnection_t_kernel(tc, x, weight, bias, mask, out):
             if c == 0 and not WFIRST:
                 load_w()
 
-        wm = const.tile([P, 2 * K], BF16, name="wm")
         wg = const.tile([P, 2 * O * 4], BF16, name="wg", align_bytes=64)
         wcodes = const.tile([P, 2 * O], U32, name="wcodes", align_bytes=64)
         wscales = const.tile([P, 2 * O], U8, name="wscales", align_bytes=64)
@@ -169,15 +168,22 @@ def tile_structuredconnection_t_kernel(tc, x, weight, bias, mask, out):
             nc.sync.dma_start(out=rows.rearrange("(p t) o -> p (t o)", t=t_cnt), in_=o_sb[c][:])
 
         def op_wm(t):
-            nc.vector.tensor_tensor(out=wm[:, t * K : (t + 1) * K], in0=w_sb[:, t, :], in1=m_sb[:, t, :], op=mult)
+            nc.vector.tensor_tensor(out=w_sb[:, t, :], in0=w_sb[:, t, :], in1=m_sb[:, t, :], op=mult)
 
         def op_tw(t):
-            transposes(("w", t), wm[:].bitcast(F32), t * (K // 2))
+            if t == 0:
+                for g in range(2):
+                    pt = ps_t.tile([P, 2, 2, P], F32, name="pt", tag="pt")
+                    bank[("w", g)] = pt
+            src32 = w_sb[:].rearrange("p t k -> p (t k)").bitcast(F32)
+            for q in range(4):
+                col0 = t * (K // 2) + q * P
+                nc.tensor.transpose(bank[("w", q // 2)][:, q % 2, t, :], src32[:, col0 : col0 + P], ident[:])
 
-        def op_cw(t):
+        def op_cw(g):
             nc.scalar.copy(
-                out=wg32[:, :, t * P : (t + 1) * P, :],
-                in_=bank[("w", t)][:].rearrange("p (g u) r -> p g r u", u=2),
+                out=wg32[:, g, :, :].rearrange("p (r t) u -> p r t u", t=2),
+                in_=bank[("w", g)][:].rearrange("p u t r -> p r t u"),
             )
 
         def op_qw(z):
@@ -211,7 +217,7 @@ def tile_structuredconnection_t_kernel(tc, x, weight, bias, mask, out):
             if kind == "TW":
                 return [("WM", v)]
             if kind == "CW":
-                return [("TW", v)]
+                return [("TW", 0), ("TW", 1)]
             if kind == "QW":
                 return [("CW", 0), ("CW", 1)]
             if kind == "BC":

from contextlib import ExitStack

import concourse.mybir as mybir
from concourse.masks import make_identity

F32 = mybir.dt.float32
BF16 = mybir.dt.bfloat16
U32 = mybir.dt.uint32
U8 = mybir.dt.uint8
FP8X4 = mybir.dt.float8_e4m3fn_x4

M, K, O = 8192, 1024, 256
P = 128
FLOPS = 2 * M * K * O

CHUNKS = [2,2,4,8,8,8,8,8,8,8]
XBIG_BUFS = 5
MANUAL = True
RP = 2
LAG = 1
QAHEAD = 3
NT = 5
GB = 4
CB = 5
WFIRST = False
NPAIR = M // P // 2


def merge(queues, deps):
    pos = [0] * len(queues)
    done = set()
    order = []
    total = sum(len(q) for q in queues)
    for sweep in range(total + 1):
        moved = False
        for qi, q in enumerate(queues):
            if pos[qi] < len(q):
                op = q[pos[qi]]
                if all(d in done for d in deps(op)):
                    order.append(op)
                    done.add(op)
                    pos[qi] += 1
                    moved = True
        if not moved:
            break
    assert len(order) == total, "the four orders contradict each other"
    return order


def tile_structuredconnection_t_kernel(tc, x, weight, bias, mask, out):
    nc = tc.nc
    mult = mybir.AluOpType.mult
    add = mybir.AluOpType.add
    with ExitStack() as ctx:
        const = ctx.enter_context(tc.tile_pool(name="const", bufs=1))
        xin = ctx.enter_context(tc.tile_pool(name="xin", bufs=1))
        stage = ctx.enter_context(tc.tile_pool(name="stage", bufs=1))
        work = ctx.enter_context(tc.tile_pool(name="work", bufs=1))
        ps_t = ctx.enter_context(tc.psum_pool(name="ps_t", bufs=NT))
        ps_o = ctx.enter_context(tc.psum_pool(name="ps_o", bufs=8 - NT))
        if MANUAL:
            ctx.enter_context(tc.manual_schedule())

        where = []
        row0 = []
        r = 0
        for c, t_cnt in enumerate(CHUNKS):
            row0.append(r)
            r += P * t_cnt
            for t in range(t_cnt):
                where.append((c, t))
        assert r == M

        x_sb = []
        o_sb = []
        w_sb = const.tile([P, 2, K], BF16, name="w_sb")
        m_sb = const.tile([P, 2, K], BF16, name="m_sb")
        brow = const.tile([P, O], BF16, name="brow")
        ones = const.tile([P, P], BF16, name="ones")
        ident = const.tile([P, P], F32, name="ident")
        nc.vector.memset(brow[:], 0.0)
        nc.vector.memset(ones[:], 1.0)
        make_identity(nc, ident[:])
        nc.scalar.dma_start(out=brow[0:1, :], in_=bias.unsqueeze(0))

        def load_w():
            nc.sync.dma_start(out=w_sb[:], in_=weight.rearrange("(p t) k -> p t k", t=2))
            nc.sync.dma_start(out=m_sb[:], in_=mask.rearrange("(p t) k -> p t k", t=2))

        if WFIRST:
            load_w()
        for c, t_cnt in enumerate(CHUNKS):
            if t_cnt == 8:
                xt_sb = xin.tile([P, t_cnt * K], BF16, name="xbig%d" % c, tag="xbig", bufs=XBIG_BUFS)
            else:
                xt_sb = xin.tile([P, t_cnt * K], BF16, name="xs%d" % c, tag="xs%d" % c)
            rows = x[row0[c] : row0[c] + P * t_cnt, :]
            nc.sync.dma_start(out=xt_sb[:], in_=rows.rearrange("(p t) k -> p (t k)", t=t_cnt))
            x_sb.append(xt_sb)
            o_sb.append(stage.tile([P, t_cnt * O], F32, name="o%d" % c, tag="o%d" % c))
            if c == 0 and not WFIRST:
                load_w()

        wg = const.tile([P, 2 * O * 4], BF16, name="wg", align_bytes=64)
        wcodes = const.tile([P, 2 * O], U32, name="wcodes", align_bytes=64)
        wscales = const.tile([P, 2 * O], U8, name="wscales", align_bytes=64)
        bias2 = const.tile([P, 2, O], F32, name="bias2")
        wg32 = wg[:].bitcast(F32).rearrange("p (g o u) -> p g o u", g=2, u=2)

        bank = {}
        grp = {}
        codes = {}
        scl = {}
        acc = {}

        def transposes(key, src32, col0):
            pt = ps_t.tile([P, 4, P], F32, name="pt", tag="pt")
            bank[key] = pt
            for q in range(4):
                nc.tensor.transpose(pt[:, q, :], src32[:, col0 + q * P : col0 + (q + 1) * P], ident[:])

        def op_t(n):
            c, t = where[n]
            transposes(("x", n), x_sb[c][:].bitcast(F32), t * (K // 2))

        def op_c(n):
            h, i = divmod(n, 2)
            if i == 0:
                grp[h] = work.tile([P, 2 * K], BF16, name="grp", tag="grp", bufs=GB, align_bytes=64)
            dst = grp[h][:].bitcast(F32)[:, i * (K // 2) : (i + 1) * (K // 2)]
            nc.scalar.copy(
                out=dst.rearrange("p (g r u) -> p g r u", g=2, u=2),
                in_=bank[("x", n)][:].rearrange("p (g u) r -> p g r u", u=2),
            )

        def op_q(h):
            codes[h] = work.tile([P, K // 2], U32, name="codes", tag="codes", bufs=CB, align_bytes=64)
            scl[h] = work.tile([P, K // 2], U8, name="scl", tag="scl", bufs=CB, align_bytes=64)
            nc.vector.quantize_mx(out=codes[h][:].bitcast(FP8X4), scales=scl[h][:], in_=grp[h][:])

        def op_x(h):
            acc[h] = ps_o.tile([P, 2, O], F32, name="acc", tag="acc")
            for i in range(2):
                for g in range(2):
                    lo = (i * 2 + g) * P
                    nc.tensor.matmul_mx(
                        out=acc[h][:, i, :],
                        lhsT=codes[h][:, lo : lo + P].bitcast(FP8X4),
                        lhsT_scale=scl[h][:, lo : lo + P],
                        rhs=wcodes[:, g * O : (g + 1) * O].bitcast(FP8X4),
                        rhs_scale=wscales[:, g * O : (g + 1) * O],
                        start=(g == 0),
                        stop=(g == 1),
                    )

        def op_a(h):
            c, t = where[2 * h]
            nc.vector.tensor_tensor(
                out=o_sb[c][:, t * O : (t + 2) * O],
                in0=acc[h][:].rearrange("p i o -> p (i o)"),
                in1=bias2[:].rearrange("p i o -> p (i o)"),
                op=add,
            )

        def op_s(c):
            t_cnt = CHUNKS[c]
            rows = out[row0[c] : row0[c] + P * t_cnt, :]
            nc.sync.dma_start(out=rows.rearrange("(p t) o -> p (t o)", t=t_cnt), in_=o_sb[c][:])

        def op_wm(t):
            nc.vector.tensor_tensor(out=w_sb[:, t, :], in0=w_sb[:, t, :], in1=m_sb[:, t, :], op=mult)

        def op_tw(t):
            if t == 0:
                for g in range(2):
                    pt = ps_t.tile([P, 2, 2, P], F32, name="pt", tag="pt")
                    bank[("w", g)] = pt
            src32 = w_sb[:].rearrange("p t k -> p (t k)").bitcast(F32)
            for q in range(4):
                col0 = t * (K // 2) + q * P
                nc.tensor.transpose(bank[("w", q // 2)][:, q % 2, t, :], src32[:, col0 : col0 + P], ident[:])

        def op_cw(g):
            nc.scalar.copy(
                out=wg32[:, g, :, :].rearrange("p (r t) u -> p r t u", t=2),
                in_=bank[("w", g)][:].rearrange("p u t r -> p r t u"),
            )

        def op_qw(z):
            nc.vector.quantize_mx(out=wcodes[:].bitcast(FP8X4), scales=wscales[:], in_=wg[:])

        def op_bm(z):
            acc["b"] = ps_o.tile([P, 2, O], F32, name="acc", tag="acc")
            nc.tensor.matmul(acc["b"][:, 0, :], lhsT=ones[:], rhs=brow[:], start=True, stop=True)

        def op_bc(z):
            for i in range(2):
                nc.vector.tensor_copy(out=bias2[:, i, :], in_=acc["b"][:, 0, :])

        emit = {"T": op_t, "C": op_c, "Q": op_q, "X": op_x, "A": op_a, "S": op_s,
                "WM": op_wm, "TW": op_tw, "CW": op_cw, "QW": op_qw, "BM": op_bm, "BC": op_bc}

        pairs_of = [[h for h in range(NPAIR) if where[2 * h][0] == c] for c in range(len(CHUNKS))]

        def deps(op):
            kind, v = op
            if kind == "C":
                return [("T", v)]
            if kind == "Q":
                return [("C", 2 * v), ("C", 2 * v + 1)]
            if kind == "X":
                return [("Q", v), ("QW", 0)]
            if kind == "A":
                return [("X", v), ("BC", 0)]
            if kind == "S":
                return [("A", h) for h in pairs_of[v]]
            if kind == "TW":
                return [("WM", v)]
            if kind == "CW":
                return [("TW", 0), ("TW", 1)]
            if kind == "QW":
                return [("CW", 0), ("CW", 1)]
            if kind == "BC":
                return [("BM", 0)]
            return []

        w_pe = [("TW", 0), ("TW", 1), ("BM", 0)]
        w_act = [("CW", 0), ("CW", 1)]
        nr = NPAIR // RP
        pe = []
        act = []
        for s in range(nr + LAG):
            if s < nr:
                for n in range(2 * RP * s, 2 * RP * (s + 1)):
                    pe.append(("T", n))
                    act.append(("C", n))
                    if n == 1 and not WFIRST:
                        pe.extend(w_pe)
                        act.extend(w_act)
            if s >= LAG:
                for h in range(RP * (s - LAG), RP * (s - LAG + 1)):
                    pe.append(("X", h))
        if WFIRST:
            pe = w_pe + pe
            act = w_act + act
        dve = [("WM", 0), ("WM", 1)]
        if not WFIRST:
            dve.append(("Q", 0))
        dve.extend([("QW", 0), ("BC", 0)])
        dve.extend([("Q", h) for h in range(0 if WFIRST else 1, QAHEAD)])
        for h in range(NPAIR):
            dve.append(("A", h))
            if h + QAHEAD < NPAIR:
                dve.append(("Q", h + QAHEAD))
        sp = [("S", c) for c in range(len(CHUNKS))]

        for kind, v in merge([pe, act, dve, sp], deps):
            emit[kind](v)
